import numpy as np
import ml_dtypes


def mxq(x, axis, fmt="e4m3"):
    dtype, down = {"e4m3": (ml_dtypes.float8_e4m3fn, 7), "e5m2": (ml_dtypes.float8_e5m2, 14)}[fmt]
    v = np.moveaxis(np.asarray(x, np.float32).astype(ml_dtypes.bfloat16).astype(np.float64), axis, -1)
    blocks = v.reshape(v.shape[:-1] + (-1, 32))
    amax = np.abs(blocks).max(-1, keepdims=True)
    byte = np.maximum(np.where(amax > 0, np.frexp(amax)[1] - 1 + 127, 0) - down, 1)
    scale = np.exp2(byte - 127.0)
    codes = (blocks / scale).astype(np.float32).astype(dtype).astype(np.float64)
    return np.moveaxis((codes * scale).reshape(v.shape), -1, axis)


WIDE = False


def mx_kscale(k):
    if not WIDE:
        return np.ones(k)
    levels = np.array([10, -10, 5, -5, 0])
    a = np.random.permutation(np.resize(levels, k // 512 * 4)).reshape(k // 512, 4)
    idx = np.arange(k)
    return np.exp2(a[idx // 512, idx % 128 // 32])


BF16 = ml_dtypes.bfloat16


def bf(x):
    return np.asarray(x, np.float32).astype(BF16)


def f64(x):
    return np.asarray(x).astype(np.float64)


B, L, D, H = 1, 1024, 512, 8


def setup_inputs():
    s = mx_kscale(D)
    return {"x": bf(np.random.standard_normal((B, L, D)) * s),
            "w": bf(np.random.standard_normal((H, D, D)) / np.sqrt(D) / s[:, None] * s[None, :])}


def reference(x, w):
    wq = mxq(f64(w), 1, "e4m3")
    xq = mxq(f64(x), 2, "e4m3")
    xs = (xq[None] @ wq[:, None]).reshape(H * B, L, D)
    return mxq(xs, 2, "e4m3") @ wq

@@ -1,0 +1,172 @@
+from contextlib import ExitStack
+
+import concourse.mybir as mybir
+from concourse.masks import make_identity
+
+BF16 = mybir.dt.bfloat16
+F32 = mybir.dt.float32
+U32 = mybir.dt.uint32
+U8 = mybir.dt.uint8
+FP8X4 = mybir.dt.float8_e4m3fn_x4
+
+P = 128
+PACK = 4
+HEADS = 8
+TOKENS = 1024
+FEATURES = P * PACK
+TOKEN_TILES = TOKENS // P
+CHUNK = 4
+CHUNKS_PER_HEAD = TOKEN_TILES // CHUNK
+CHUNKS = HEADS * CHUNKS_PER_HEAD
+CHUNK_TOKENS = CHUNK * P
+SCALAR_XS_BANKS = 1
+STORE_TILES = 2
+
+FLOPS = 2 * 2 * HEADS * TOKENS * FEATURES * FEATURES
+
+
+def tile_multiheadattention_pa_kernel(tc, x, w, out):
+    nc = tc.nc
+    x_tiles = x[0].rearrange("(c r) k -> c r k", r=TOKEN_TILES)
+
+    with ExitStack() as ctx:
+        keep = ctx.enter_context(tc.tile_pool(name="keep", bufs=1))
+        stage = ctx.enter_context(tc.tile_pool(name="stage", bufs=2))
+        store = ctx.enter_context(tc.tile_pool(name="store", bufs=6))
+        psum = ctx.enter_context(tc.psum_pool(name="psum", bufs=CHUNK))
+        ctx.enter_context(tc.manual_schedule())
+
+        x_rows = keep.tile([P, TOKEN_TILES, FEATURES], BF16)
+        w_rows = [keep.tile([P, PACK, FEATURES], BF16, name="w_rows%d" % h) for h in range(HEADS)]
+
+        def load_x(half):
+            tiles = slice(half * CHUNK, (half + 1) * CHUNK)
+            nc.sync.dma_start(out=x_rows[:, tiles, :], in_=x_tiles[:, tiles, :])
+
+        def load_w(h):
+            nc.sync.dma_start(out=w_rows[h][:], in_=w[h].rearrange("(t p) n -> p t n", p=P))
+
+        load_x(0)
+        load_w(0)
+        load_x(1)
+        for h in range(1, HEADS):
+            load_w(h)
+
+        identity = keep.tile([P, P], BF16)
+        make_identity(nc, identity[:])
+
+        w_codes = [keep.tile([P, FEATURES], U32, name="w_codes%d" % h, align_bytes=64) for h in range(HEADS)]
+        w_scales = [keep.tile([P, FEATURES], U8, name="w_scales%d" % h, align_bytes=64) for h in range(HEADS)]
+        w_grouped = {}
+
+        def regroup_w(h):
+            w_grouped[h] = stage.tile([P, FEATURES, PACK], BF16, name="w_grouped", align_bytes=64)
+            nc.vector.tensor_copy(
+                out=w_grouped[h][:].rearrange("p (c i) t -> p c t i", i=4),
+                in_=w_rows[h][:].rearrange("p t (c i) -> p c t i", i=4),
+            )
+
+        def quantise_w(h):
+            nc.vector.quantize_mx(
+                out=w_codes[h][:].bitcast(FP8X4),
+                scales=w_scales[h][:],
+                in_=w_grouped[h][:].rearrange("p n t -> p (n t)"),
+            )
+
+        x_grouped = keep.tile([P, TOKEN_TILES, P, PACK], BF16, align_bytes=64)
+        x_codes = keep.tile([P, TOKENS], U32, align_bytes=64)
+        x_scales = keep.tile([P, TOKENS], U8, align_bytes=64)
+
+        def transpose_x(r):
+            x_bank = psum.tile([P, PACK, P], BF16, tag="xs_bank" if r < CHUNK else "out_bank")
+            for t in range(PACK):
+                nc.tensor.transpose(x_bank[:, t, :], x_rows[:, r, t * P : (t + 1) * P], identity[:])
+            nc.scalar.copy(out=x_grouped[:, r, :, :], in_=x_bank[:].rearrange("p t c -> p c t"))
+
+        def quantise_x(half):
+            tiles = slice(half * CHUNK, (half + 1) * CHUNK)
+            tokens = slice(half * CHUNK_TOKENS, (half + 1) * CHUNK_TOKENS)
+            nc.vector.quantize_mx(
+                out=x_codes[:, tokens].bitcast(FP8X4),
+                scales=x_scales[:, tokens],
+                in_=x_grouped[:, tiles, :, :].rearrange("p r c t -> p (r c t)"),
+            )
+
+        def first_matmul(j, i):
+            h = j // CHUNKS_PER_HEAD
+            r = (j % CHUNKS_PER_HEAD) * CHUNK + i
+            tokens = slice(r * P, (r + 1) * P)
+            xs_bank = psum.tile([P, PACK, P], F32, tag="xs_bank")
+            for t in range(PACK):
+                features = slice(t * P, (t + 1) * P)
+                nc.tensor.matmul_mx(
+                    out=xs_bank[:, t, :],
+                    lhsT=w_codes[h][:, features].bitcast(FP8X4),
+                    lhsT_scale=w_scales[h][:, features],
+                    rhs=x_codes[:, tokens].bitcast(FP8X4),
+                    rhs_scale=x_scales[:, tokens],
+                    start=True,
+                    stop=True,
+                )
+            return xs_bank
+
+        def second_matmul(j, i, xs_codes, xs_scales):
+            h = j // CHUNKS_PER_HEAD
+            tokens = slice(i * P, (i + 1) * P)
+            out_bank = psum.tile([P, FEATURES], F32, tag="out_bank")
+            nc.tensor.matmul_mx(
+                out=out_bank[:],
+                lhsT=xs_codes[:, tokens].bitcast(FP8X4),
+                lhsT_scale=xs_scales[:, tokens],
+                rhs=w_codes[h][:].bitcast(FP8X4),
+                rhs_scale=w_scales[h][:],
+                start=True,
+                stop=True,
+            )
+            return out_bank
+
+        def store_chunk(j, out_banks):
+            h = j // CHUNKS_PER_HEAD
+            out_tiles = out[h].rearrange("(c r) e -> c r e", r=TOKEN_TILES)
+            for first in range(0, CHUNK, STORE_TILES):
+                out_rows = store.tile([P, STORE_TILES, FEATURES], F32)
+                for s in range(STORE_TILES):
+                    nc.scalar.copy(out=out_rows[:, s, :], in_=out_banks[first + s][:])
+                r = (j % CHUNKS_PER_HEAD) * CHUNK + first
+                nc.sync.dma_start(out=out_tiles[:, r : r + STORE_TILES, :], in_=out_rows[:])
+
+        for r in range(TOKEN_TILES):
+            transpose_x(r)
+        regroup_w(0)
+        quantise_w(0)
+        quantise_x(0)
+        regroup_w(1)
+        quantise_x(1)
+        xs_banks = [first_matmul(0, i) for i in range(CHUNK)]
+        out_banks = []
+
+        for j in range(CHUNKS):
+            h = j // CHUNKS_PER_HEAD
+            xs_grouped = stage.tile([P, CHUNK, P, PACK], BF16, align_bytes=64)
+            xs_codes = stage.tile([P, CHUNK_TOKENS], U32, align_bytes=64)
+            xs_scales = stage.tile([P, CHUNK_TOKENS], U8, align_bytes=64)
+            next_xs_banks = []
+            for i in range(CHUNK):
+                copy = nc.scalar.copy if i < SCALAR_XS_BANKS else nc.vector.tensor_copy
+                copy(out=xs_grouped[:, i, :, :], in_=xs_banks[i][:].rearrange("p t c -> p c t"))
+                if j + 1 < CHUNKS:
+                    next_xs_banks.append(first_matmul(j + 1, i))
+                if i + 1 == SCALAR_XS_BANKS and j > 0:
+                    store_chunk(j - 1, out_banks)
+            if j % CHUNKS_PER_HEAD == 0 and h + 1 < HEADS:
+                quantise_w(h + 1)
+            if j % CHUNKS_PER_HEAD == 1 and h + 2 < HEADS:
+                regroup_w(h + 2)
+            nc.vector.quantize_mx(
+                out=xs_codes[:].bitcast(FP8X4),
+                scales=xs_scales[:],
+                in_=xs_grouped[:].rearrange("p i c t -> p (i c t)"),
+            )
+            out_banks = [second_matmul(j, i, xs_codes, xs_scales) for i in range(CHUNK)]
+            xs_banks = next_xs_banks
+        store_chunk(CHUNKS - 1, out_banks)

@@ -21,6 +21,8 @@ CHUNKS = HEADS * CHUNKS_PER_HEAD
 CHUNK_TOKENS = CHUNK * P
 SCALAR_XS_BANKS = 1
 STORE_TILES = 2
+W_HALF = FEATURES // 2
+W_HALVES = 2 * HEADS
 
 FLOPS = 2 * 2 * HEADS * TOKENS * FEATURES * FEATURES
 
@@ -57,20 +59,29 @@ def tile_multiheadattention_pa_kernel(tc, x, w, out):
 
         w_codes = [keep.tile([P, FEATURES], U32, name="w_codes%d" % h, align_bytes=64) for h in range(HEADS)]
         w_scales = [keep.tile([P, FEATURES], U8, name="w_scales%d" % h, align_bytes=64) for h in range(HEADS)]
-        w_grouped = {}
+        w_grouped = [keep.tile([P, W_HALF, PACK], BF16, name="w_grouped%d" % s, align_bytes=64) for s in range(2)]
 
-        def regroup_w(h):
-            w_grouped[h] = stage.tile([P, FEATURES, PACK], BF16, name="w_grouped", align_bytes=64)
-            nc.vector.tensor_copy(
-                out=w_grouped[h][:].rearrange("p (c i) t -> p c t i", i=4),
-                in_=w_rows[h][:].rearrange("p t (c i) -> p c t i", i=4),
-            )
+        def regroup_w(m, on_gpsimd):
+            columns = slice((m % 2) * W_HALF, (m % 2 + 1) * W_HALF)
+            rows = w_rows[m // 2][:, :, columns].rearrange("p t n -> p n t")
+            if on_gpsimd:
+                nc.gpsimd.tensor_scalar(
+                    out=w_grouped[m % 2][:],
+                    in0=rows,
+                    scalar1=1.0,
+                    scalar2=0.0,
+                    op0=mybir.AluOpType.mult,
+                    op1=mybir.AluOpType.add,
+                )
+            else:
+                nc.vector.tensor_copy(out=w_grouped[m % 2][:], in_=rows)
 
-        def quantise_w(h):
+        def quantise_w(m):
+            columns = slice((m % 2) * W_HALF, (m % 2 + 1) * W_HALF)
             nc.vector.quantize_mx(
-                out=w_codes[h][:].bitcast(FP8X4),
-                scales=w_scales[h][:],
-                in_=w_grouped[h][:].rearrange("p n t -> p (n t)"),
+                out=w_codes[m // 2][:, columns].bitcast(FP8X4),
+                scales=w_scales[m // 2][:, columns],
+                in_=w_grouped[m % 2][:].rearrange("p n t -> p (n t)"),
             )
 
         x_grouped = keep.tile([P, TOKEN_TILES, P, PACK], BF16, align_bytes=64)
@@ -125,28 +136,32 @@ def tile_multiheadattention_pa_kernel(tc, x, w, out):
             )
             return out_bank
 
-        def store_chunk(j, out_banks):
+        def store_chunk(j, out_banks, copies):
             h = j // CHUNKS_PER_HEAD
             out_tiles = out[h].rearrange("(c r) e -> c r e", r=TOKEN_TILES)
             for first in range(0, CHUNK, STORE_TILES):
                 out_rows = store.tile([P, STORE_TILES, FEATURES], F32)
                 for s in range(STORE_TILES):
-                    nc.scalar.copy(out=out_rows[:, s, :], in_=out_banks[first + s][:])
+                    copies[(first + s) % len(copies)](out=out_rows[:, s, :], in_=out_banks[first + s][:])
                 r = (j % CHUNKS_PER_HEAD) * CHUNK + first
                 nc.sync.dma_start(out=out_tiles[:, r : r + STORE_TILES, :], in_=out_rows[:])
 
         for r in range(TOKEN_TILES):
             transpose_x(r)
-        regroup_w(0)
+        regroup_w(0, on_gpsimd=False)
+        regroup_w(1, on_gpsimd=False)
         quantise_w(0)
+        quantise_w(1)
         quantise_x(0)
-        regroup_w(1)
+        regroup_w(2, on_gpsimd=False)
+        regroup_w(3, on_gpsimd=False)
         quantise_x(1)
+        quantise_w(2)
+        regroup_w(4, on_gpsimd=True)
         xs_banks = [first_matmul(0, i) for i in range(CHUNK)]
         out_banks = []
 
         for j in range(CHUNKS):
-            h = j // CHUNKS_PER_HEAD
             xs_grouped = stage.tile([P, CHUNK, P, PACK], BF16, align_bytes=64)
             xs_codes = stage.tile([P, CHUNK_TOKENS], U32, align_bytes=64)
             xs_scales = stage.tile([P, CHUNK_TOKENS], U8, align_bytes=64)
@@ -157,11 +172,11 @@ def tile_multiheadattention_pa_kernel(tc, x, w, out):
                 if j + 1 < CHUNKS:
                     next_xs_banks.append(first_matmul(j + 1, i))
                 if i + 1 == SCALAR_XS_BANKS and j > 0:
-                    store_chunk(j - 1, out_banks)
-            if j % CHUNKS_PER_HEAD == 0 and h + 1 < HEADS:
-                quantise_w(h + 1)
-            if j % CHUNKS_PER_HEAD == 1 and h + 2 < HEADS:
-                regroup_w(h + 2)
+                    store_chunk(j - 1, out_banks, [nc.scalar.copy])
+            if j + 3 < W_HALVES:
+                quantise_w(j + 3)
+            if j + 5 < W_HALVES:
+                regroup_w(j + 5, on_gpsimd=True)
             nc.vector.quantize_mx(
                 out=xs_codes[:].bitcast(FP8X4),
                 scales=xs_scales[:],
@@ -169,4 +184,4 @@ def tile_multiheadattention_pa_kernel(tc, x, w, out):
             )
             out_banks = [second_matmul(j, i, xs_codes, xs_scales) for i in range(CHUNK)]
             xs_banks = next_xs_banks
-        store_chunk(CHUNKS - 1, out_banks)
+        store_chunk(CHUNKS - 1, out_banks, [nc.scalar.copy, nc.vector.tensor_copy])

@@ -19,8 +19,7 @@ CHUNK = 4
 CHUNKS_PER_HEAD = TOKEN_TILES // CHUNK
 CHUNKS = HEADS * CHUNKS_PER_HEAD
 CHUNK_TOKENS = CHUNK * P
-SCALAR_XS_BANKS = 1
-STORE_TILES = 2
+VECTOR_ALONE_EVERY = 4
 W_HALF = FEATURES // 2
 W_HALVES = 2 * HEADS
 
@@ -34,7 +33,7 @@ def tile_multiheadattention_pa_kernel(tc, x, w, out):
     with ExitStack() as ctx:
         keep = ctx.enter_context(tc.tile_pool(name="keep", bufs=1))
         stage = ctx.enter_context(tc.tile_pool(name="stage", bufs=2))
-        store = ctx.enter_context(tc.tile_pool(name="store", bufs=6))
+        store = ctx.enter_context(tc.tile_pool(name="store", bufs=12))
         psum = ctx.enter_context(tc.psum_pool(name="psum", bufs=CHUNK))
         ctx.enter_context(tc.manual_schedule())
 
@@ -63,18 +62,21 @@ def tile_multiheadattention_pa_kernel(tc, x, w, out):
 
         def regroup_w(m, on_gpsimd):
             columns = slice((m % 2) * W_HALF, (m % 2 + 1) * W_HALF)
-            rows = w_rows[m // 2][:, :, columns].rearrange("p t n -> p n t")
+            rows = w_rows[m // 2][:, :, columns]
             if on_gpsimd:
                 nc.gpsimd.tensor_scalar(
                     out=w_grouped[m % 2][:],
-                    in0=rows,
+                    in0=rows.rearrange("p t n -> p n t"),
                     scalar1=1.0,
                     scalar2=0.0,
                     op0=mybir.AluOpType.mult,
                     op1=mybir.AluOpType.add,
                 )
             else:
-                nc.vector.tensor_copy(out=w_grouped[m % 2][:], in_=rows)
+                nc.vector.tensor_copy(
+                    out=w_grouped[m % 2][:].rearrange("p (c i) t -> p c t i", i=4),
+                    in_=rows.rearrange("p t (c i) -> p c t i", i=4),
+                )
 
         def quantise_w(m):
             columns = slice((m % 2) * W_HALF, (m % 2 + 1) * W_HALF)
@@ -139,12 +141,10 @@ def tile_multiheadattention_pa_kernel(tc, x, w, out):
         def store_chunk(j, out_banks, copies):
             h = j // CHUNKS_PER_HEAD
             out_tiles = out[h].rearrange("(c r) e -> c r e", r=TOKEN_TILES)
-            for first in range(0, CHUNK, STORE_TILES):
-                out_rows = store.tile([P, STORE_TILES, FEATURES], F32)
-                for s in range(STORE_TILES):
-                    copies[(first + s) % len(copies)](out=out_rows[:, s, :], in_=out_banks[first + s][:])
-                r = (j % CHUNKS_PER_HEAD) * CHUNK + first
-                nc.sync.dma_start(out=out_tiles[:, r : r + STORE_TILES, :], in_=out_rows[:])
+            for i in range(CHUNK):
+                out_rows = store.tile([P, FEATURES], F32)
+                copies[i % len(copies)](out=out_rows[:], in_=out_banks[i][:])
+                nc.sync.dma_start(out=out_tiles[:, (j % CHUNKS_PER_HEAD) * CHUNK + i, :], in_=out_rows[:])
 
         for r in range(TOKEN_TILES):
             transpose_x(r)
@@ -166,13 +166,14 @@ def tile_multiheadattention_pa_kernel(tc, x, w, out):
             xs_codes = stage.tile([P, CHUNK_TOKENS], U32, align_bytes=64)
             xs_scales = stage.tile([P, CHUNK_TOKENS], U8, align_bytes=64)
             next_xs_banks = []
+            scalar_xs_banks = 0 if j % VECTOR_ALONE_EVERY == VECTOR_ALONE_EVERY - 1 else 1
             for i in range(CHUNK):
-                copy = nc.scalar.copy if i < SCALAR_XS_BANKS else nc.vector.tensor_copy
+                if i == scalar_xs_banks and j > 0:
+                    store_chunk(j - 1, out_banks, [nc.scalar.copy])
+                copy = nc.scalar.copy if i < scalar_xs_banks else nc.vector.tensor_copy
                 copy(out=xs_grouped[:, i, :, :], in_=xs_banks[i][:].rearrange("p t c -> p c t"))
                 if j + 1 < CHUNKS:
                     next_xs_banks.append(first_matmul(j + 1, i))
-                if i + 1 == SCALAR_XS_BANKS and j > 0:
-                    store_chunk(j - 1, out_banks, [nc.scalar.copy])
             if j + 3 < W_HALVES:
                 quantise_w(j + 3)
             if j + 5 < W_HALVES:

@@ -19,7 +19,9 @@ CHUNK = 4
 CHUNKS_PER_HEAD = TOKEN_TILES // CHUNK
 CHUNKS = HEADS * CHUNKS_PER_HEAD
 CHUNK_TOKENS = CHUNK * P
-VECTOR_ALONE_EVERY = 4
+SCALAR_XS_BANKS = 1
+SCALAR_XS_BANKS_FIRST_ROUND = 3
+SCALAR_XS_BANKS_LAST_ROUND = 0
 W_HALF = FEATURES // 2
 W_HALVES = 2 * HEADS
 
@@ -155,9 +157,9 @@ def tile_multiheadattention_pa_kernel(tc, x, w, out):
         quantise_x(0)
         regroup_w(2, on_gpsimd=False)
         regroup_w(3, on_gpsimd=False)
-        quantise_x(1)
         quantise_w(2)
-        regroup_w(4, on_gpsimd=True)
+        quantise_x(1)
+        regroup_w(4, on_gpsimd=False)
         xs_banks = [first_matmul(0, i) for i in range(CHUNK)]
         out_banks = []
 
@@ -166,7 +168,11 @@ def tile_multiheadattention_pa_kernel(tc, x, w, out):
             xs_codes = stage.tile([P, CHUNK_TOKENS], U32, align_bytes=64)
             xs_scales = stage.tile([P, CHUNK_TOKENS], U8, align_bytes=64)
             next_xs_banks = []
-            scalar_xs_banks = 0 if j % VECTOR_ALONE_EVERY == VECTOR_ALONE_EVERY - 1 else 1
+            scalar_xs_banks = SCALAR_XS_BANKS
+            if j == 0:
+                scalar_xs_banks = SCALAR_XS_BANKS_FIRST_ROUND
+            if j == CHUNKS - 1:
+                scalar_xs_banks = SCALAR_XS_BANKS_LAST_ROUND
             for i in range(CHUNK):
                 if i == scalar_xs_banks and j > 0:
                     store_chunk(j - 1, out_banks, [nc.scalar.copy])

from contextlib import ExitStack

import concourse.mybir as mybir
from concourse.masks import make_identity

BF16 = mybir.dt.bfloat16
F32 = mybir.dt.float32
U32 = mybir.dt.uint32
U8 = mybir.dt.uint8
FP8X4 = mybir.dt.float8_e4m3fn_x4

P = 128
PACK = 4
HEADS = 8
TOKENS = 1024
FEATURES = P * PACK
TOKEN_TILES = TOKENS // P
CHUNK = 4
CHUNKS_PER_HEAD = TOKEN_TILES // CHUNK
CHUNKS = HEADS * CHUNKS_PER_HEAD
CHUNK_TOKENS = CHUNK * P
SCALAR_XS_BANKS = 1
SCALAR_XS_BANKS_FIRST_ROUND = 3
SCALAR_XS_BANKS_LAST_ROUND = 0
W_HALF = FEATURES // 2
W_HALVES = 2 * HEADS

FLOPS = 2 * 2 * HEADS * TOKENS * FEATURES * FEATURES


def tile_multiheadattention_pa_kernel(tc, x, w, out):
    nc = tc.nc
    x_tiles = x[0].rearrange("(c r) k -> c r k", r=TOKEN_TILES)

    with ExitStack() as ctx:
        keep = ctx.enter_context(tc.tile_pool(name="keep", bufs=1))
        stage = ctx.enter_context(tc.tile_pool(name="stage", bufs=2))
        store = ctx.enter_context(tc.tile_pool(name="store", bufs=12))
        psum = ctx.enter_context(tc.psum_pool(name="psum", bufs=CHUNK))
        ctx.enter_context(tc.manual_schedule())

        x_rows = keep.tile([P, TOKEN_TILES, FEATURES], BF16)
        w_rows = [keep.tile([P, PACK, FEATURES], BF16, name="w_rows%d" % h) for h in range(HEADS)]

        def load_x(half):
            tiles = slice(half * CHUNK, (half + 1) * CHUNK)
            nc.sync.dma_start(out=x_rows[:, tiles, :], in_=x_tiles[:, tiles, :])

        def load_w(h):
            nc.sync.dma_start(out=w_rows[h][:], in_=w[h].rearrange("(t p) n -> p t n", p=P))

        load_x(0)
        load_w(0)
        load_x(1)
        for h in range(1, HEADS):
            load_w(h)

        identity = keep.tile([P, P], BF16)
        make_identity(nc, identity[:])

        w_codes = [keep.tile([P, FEATURES], U32, name="w_codes%d" % h, align_bytes=64) for h in range(HEADS)]
        w_scales = [keep.tile([P, FEATURES], U8, name="w_scales%d" % h, align_bytes=64) for h in range(HEADS)]
        w_grouped = [keep.tile([P, W_HALF, PACK], BF16, name="w_grouped%d" % s, align_bytes=64) for s in range(2)]

        def regroup_w(m, on_gpsimd):
            columns = slice((m % 2) * W_HALF, (m % 2 + 1) * W_HALF)
            rows = w_rows[m // 2][:, :, columns]
            if on_gpsimd:
                nc.gpsimd.tensor_scalar(
                    out=w_grouped[m % 2][:],
                    in0=rows.rearrange("p t n -> p n t"),
                    scalar1=1.0,
                    scalar2=0.0,
                    op0=mybir.AluOpType.mult,
                    op1=mybir.AluOpType.add,
                )
            else:
                nc.vector.tensor_copy(
                    out=w_grouped[m % 2][:].rearrange("p (c i) t -> p c t i", i=4),
                    in_=rows.rearrange("p t (c i) -> p c t i", i=4),
                )

        def quantise_w(m):
            columns = slice((m % 2) * W_HALF, (m % 2 + 1) * W_HALF)
            nc.vector.quantize_mx(
                out=w_codes[m // 2][:, columns].bitcast(FP8X4),
                scales=w_scales[m // 2][:, columns],
                in_=w_grouped[m % 2][:].rearrange("p n t -> p (n t)"),
            )

        x_grouped = keep.tile([P, TOKEN_TILES, P, PACK], BF16, align_bytes=64)
        x_codes = keep.tile([P, TOKENS], U32, align_bytes=64)
        x_scales = keep.tile([P, TOKENS], U8, align_bytes=64)

        def transpose_x(r):
            x_bank = psum.tile([P, PACK, P], BF16, tag="xs_bank" if r < CHUNK else "out_bank")
            for t in range(PACK):
                nc.tensor.transpose(x_bank[:, t, :], x_rows[:, r, t * P : (t + 1) * P], identity[:])
            nc.scalar.copy(out=x_grouped[:, r, :, :], in_=x_bank[:].rearrange("p t c -> p c t"))

        def quantise_x(half):
            tiles = slice(half * CHUNK, (half + 1) * CHUNK)
            tokens = slice(half * CHUNK_TOKENS, (half + 1) * CHUNK_TOKENS)
            nc.vector.quantize_mx(
                out=x_codes[:, tokens].bitcast(FP8X4),
                scales=x_scales[:, tokens],
                in_=x_grouped[:, tiles, :, :].rearrange("p r c t -> p (r c t)"),
            )

        def first_matmul(j, i):
            h = j // CHUNKS_PER_HEAD
            r = (j % CHUNKS_PER_HEAD) * CHUNK + i
            tokens = slice(r * P, (r + 1) * P)
            xs_bank = psum.tile([P, PACK, P], F32, tag="xs_bank")
            for t in range(PACK):
                features = slice(t * P, (t + 1) * P)
                nc.tensor.matmul_mx(
                    out=xs_bank[:, t, :],
                    lhsT=w_codes[h][:, features].bitcast(FP8X4),
                    lhsT_scale=w_scales[h][:, features],
                    rhs=x_codes[:, tokens].bitcast(FP8X4),
                    rhs_scale=x_scales[:, tokens],
                    start=True,
                    stop=True,
                )
            return xs_bank

        def second_matmul(j, i, xs_codes, xs_scales):
            h = j // CHUNKS_PER_HEAD
            tokens = slice(i * P, (i + 1) * P)
            out_bank = psum.tile([P, FEATURES], F32, tag="out_bank")
            nc.tensor.matmul_mx(
                out=out_bank[:],
                lhsT=xs_codes[:, tokens].bitcast(FP8X4),
                lhsT_scale=xs_scales[:, tokens],
                rhs=w_codes[h][:].bitcast(FP8X4),
                rhs_scale=w_scales[h][:],
                start=True,
                stop=True,
            )
            return out_bank

        def store_chunk(j, out_banks, copies):
            h = j // CHUNKS_PER_HEAD
            out_tiles = out[h].rearrange("(c r) e -> c r e", r=TOKEN_TILES)
            for i in range(CHUNK):
                out_rows = store.tile([P, FEATURES], F32)
                copies[i % len(copies)](out=out_rows[:], in_=out_banks[i][:])
                nc.sync.dma_start(out=out_tiles[:, (j % CHUNKS_PER_HEAD) * CHUNK + i, :], in_=out_rows[:])

        for r in range(TOKEN_TILES):
            transpose_x(r)
        regroup_w(0, on_gpsimd=False)
        regroup_w(1, on_gpsimd=False)
        quantise_w(0)
        quantise_w(1)
        quantise_x(0)
        regroup_w(2, on_gpsimd=False)
        regroup_w(3, on_gpsimd=False)
        quantise_w(2)
        quantise_x(1)
        regroup_w(4, on_gpsimd=False)
        xs_banks = [first_matmul(0, i) for i in range(CHUNK)]
        out_banks = []

        for j in range(CHUNKS):
            xs_grouped = stage.tile([P, CHUNK, P, PACK], BF16, align_bytes=64)
            xs_codes = stage.tile([P, CHUNK_TOKENS], U32, align_bytes=64)
            xs_scales = stage.tile([P, CHUNK_TOKENS], U8, align_bytes=64)
            next_xs_banks = []
            scalar_xs_banks = SCALAR_XS_BANKS
            if j == 0:
                scalar_xs_banks = SCALAR_XS_BANKS_FIRST_ROUND
            if j == CHUNKS - 1:
                scalar_xs_banks = SCALAR_XS_BANKS_LAST_ROUND
            for i in range(CHUNK):
                if i == scalar_xs_banks and j > 0:
                    store_chunk(j - 1, out_banks, [nc.scalar.copy])
                copy = nc.scalar.copy if i < scalar_xs_banks else nc.vector.tensor_copy
                copy(out=xs_grouped[:, i, :, :], in_=xs_banks[i][:].rearrange("p t c -> p c t"))
                if j + 1 < CHUNKS:
                    next_xs_banks.append(first_matmul(j + 1, i))
            if j + 3 < W_HALVES:
                quantise_w(j + 3)
            if j + 5 < W_HALVES:
                regroup_w(j + 5, on_gpsimd=True)
            nc.vector.quantize_mx(
                out=xs_codes[:].bitcast(FP8X4),
                scales=xs_scales[:],
                in_=xs_grouped[:].rearrange("p i c t -> p (i c t)"),
            )
            out_banks = [second_matmul(j, i, xs_codes, xs_scales) for i in range(CHUNK)]
            xs_banks = next_xs_banks
        store_chunk(CHUNKS - 1, out_banks, [nc.scalar.copy, nc.vector.tensor_copy])
